import numpy as np
import ml_dtypes


BF16 = ml_dtypes.bfloat16


def bf(x):
    return np.asarray(x, np.float32).astype(BF16)


def f64(x):
    return np.asarray(x).astype(np.float64)


E2M1 = np.array([0.0, 0.5, 1.0, 1.5, 2.0, 3.0, 4.0, 6.0, -0.0, -0.5, -1.0, -1.5, -2.0, -3.0, -4.0, -6.0])


def pack_weight(w, fmt):
    k, n = w.shape
    w = f64(bf(w)).reshape(k // 32, 32, n)
    amax = np.abs(w).max(1)
    if fmt == "e4m3":
        byte = np.frexp(amax)[1] - 1 + 127 - 7
    else:
        mant, ex = np.frexp(amax / 6.0)
        byte = np.where(mant > 0.5, ex, ex - 1) + 127
    byte = np.clip(np.where(amax > 0, byte, 1), 1, 254)
    scaled = (w * np.exp2(127.0 - byte)[:, None, :]).reshape(k, n).astype(np.float32)
    by_word = np.ascontiguousarray(scaled.reshape(k // 512, 128, 4, n).transpose(0, 1, 3, 2))
    if fmt == "e4m3":
        words = by_word.astype(ml_dtypes.float8_e4m3fn).view(np.uint8)
    else:
        c = by_word.astype(ml_dtypes.float4_e2m1fn).view(np.uint8) & 0xF
        words = c[..., 0::2] | (c[..., 1::2] << 4)
    return np.ascontiguousarray(words), np.ascontiguousarray(byte.astype(np.uint8).reshape(k // 512, 16, n))


def unpack_weight(words, scales, fmt):
    g, p, n, _ = words.shape
    if fmt == "e4m3":
        vals = np.ascontiguousarray(words).view(ml_dtypes.float8_e4m3fn).astype(np.float64)
    else:
        nib = np.empty((g, p, n, 4), np.uint8)
        nib[..., 0::2] = words & 0xF
        nib[..., 1::2] = words >> 4
        vals = E2M1[nib]
    vals = vals * np.repeat(np.exp2(scales.astype(np.float64) - 127.0), 8, axis=1)[..., None]
    return vals.transpose(0, 1, 3, 2).reshape(g * 512, n)

def pack4(w):
    words, scales = pack_weight(w, "e2m1")
    return words.reshape(words.shape[0], 128, -1), scales


def unpack4(words, scales):
    return unpack_weight(words.reshape(words.shape[0], 128, -1, 2), scales, "e2m1")


def kspread(k):
    return np.exp2(np.repeat(np.random.randint(-6, 7, k // 32), 32).astype(np.float64))


B, K, F, INCH, OUTCH, R = 2, 4, 128, 8192, 512, 128


def erf(a):
    c = np.clip(a, -6.0, 6.0)
    c2 = 2.0 * c * c
    t = c.copy()
    s = c.copy()
    n = 1.0
    while np.max(np.abs(t) - 1e-18 * np.abs(s)) > 0.0:
        n += 2.0
        t = t * c2 / n
        s = s + t
    return 2.0 / np.sqrt(np.pi) * np.exp(-c * c) * s


def gelu(t):
    return 0.5 * t * (1.0 + erf(t / np.sqrt(2.0)))


def setup_inputs():
    s = kspread(INCH)
    h = gelu(np.random.standard_normal((B, K, F, INCH))) * s
    h_words, h_scales = pack4(np.ascontiguousarray(h.reshape(B * K * F, INCH).T))
    z = bf(np.random.standard_normal((B, K, F, R)) * 0.35)
    u = bf(np.random.standard_normal((B, K, OUTCH, R)) * 1.5 * np.sqrt(R))
    b = bf(np.random.standard_normal((B, 1, 1, OUTCH)) * 0.3)
    w = np.random.standard_normal((OUTCH, INCH)) * 1.5 / np.sqrt(INCH) / s
    words, scales = pack4(np.ascontiguousarray(w.T))
    b_out = bf(np.random.standard_normal(OUTCH) * 0.3)
    return {
        "h_words": h_words,
        "h_scales": h_scales,
        "z": z,
        "u": u,
        "b": b,
        "W_out_words": words,
        "W_out_scales": scales,
        "b_out": b_out,
    }


def reference(h_words, h_scales, z, u, b, W_out_words, W_out_scales, b_out):
    lora = f64(z) @ f64(u).transpose(0, 1, 3, 2) / R
    hq = unpack4(h_words, h_scales).T.reshape(B, K, F, INCH)
    main = hq @ unpack4(W_out_words, W_out_scales)
    return gelu(main + f64(b_out) + lora + f64(b))

@@ -1,0 +1,263 @@
+from contextlib import ExitStack
+
+import concourse.mybir as mybir
+from concourse.masks import make_identity
+
+F32 = mybir.dt.float32
+BF16 = mybir.dt.bfloat16
+I32 = mybir.dt.int32
+U8 = mybir.dt.uint8
+FP4X4 = mybir.dt.float4_e2m1fn_x4
+ACT = mybir.ActivationFunctionType
+ALU = mybir.AluOpType
+
+P = 128
+TILES = 8
+PASSES = 16
+CH = 512
+HALF = CH // 2
+ROWS = 1024
+RANK = 128
+FLOPS = 2 * ROWS * 8192 * CH + 2 * ROWS * RANK * CH
+
+RUNS = ((0, 3), (3, 7), (7, 11), (11, 16))
+W_LOADS = ((0, 1), (1, 2), (2, 4), (4, 6), (6, 8), (8, 10), (10, 12), (12, 14), (14, 16))
+SWEEP = 13
+WARM = 3
+LATE = 3
+
+
+def tile_loratacmlp4_pb_kernel(tc, h_words, h_scales, z, u, b, W_out_words, W_out_scales, b_out, out):
+    nc = tc.nc
+    with ExitStack() as ctx:
+        keep = ctx.enter_context(tc.tile_pool(name="keep", bufs=1))
+        work = ctx.enter_context(tc.tile_pool(name="work", bufs=3))
+        psum = ctx.enter_context(tc.psum_pool(name="psum", bufs=1))
+        ctx.enter_context(tc.manual_schedule())
+
+        def bank(k, width, dtype, name):
+            return psum.tile([P, width], dtype, tag="bank%d" % k, name=name)
+
+        zeros = keep.tile([P, CH], BF16, name="zeros")
+        ones = keep.tile([P, P], BF16, name="ones")
+        ident = keep.tile([P, P], BF16, name="ident")
+        brow = keep.tile([P, 2 * CH], BF16, name="brow")
+        junk = keep.tile([P, 1], F32, name="junk")
+        z_sb = keep.tile([P, 2, CH], BF16, name="z_sb")
+        zT = keep.tile([P, TILES * P], BF16, name="zT")
+        bias_sb = keep.tile([P, 2, CH], F32, name="bias_sb")
+        u_sb = []
+        for j in range(TILES // 2):
+            u_pair = keep.tile([P, 2, CH], BF16, name="u_sb%d" % j)
+            u_sb.append(u_pair)
+        h_planes = []
+        w_planes = []
+        for r, (g0, g1) in enumerate(RUNS):
+            hp = keep.tile([P, g1 - g0, ROWS], U8, name="h_planes%d" % r, align_bytes=64)
+            wp = keep.tile([P, g1 - g0, CH], U8, name="w_planes%d" % r, align_bytes=64)
+            h_planes.append(hp)
+            w_planes.append(wp)
+        h_codes = []
+        w_codes = []
+        for g in range(PASSES):
+            hc = keep.tile([P, 2 * ROWS], U8, name="h_codes%d" % g, align_bytes=64)
+            h_codes.append(hc)
+        for g0, g1 in W_LOADS:
+            wc = keep.tile([P, g1 - g0, 2 * CH], U8, name="w_codes%d" % g0, align_bytes=64)
+            for g in range(g0, g1):
+                w_codes.append((wc, g - g0))
+        run_of = {}
+        for r, (g0, g1) in enumerate(RUNS):
+            for g in range(g0, g1):
+                run_of[g] = (r, g - g0)
+
+        u_view = u.rearrange("b m (p e) r -> p (b m) (e r)", e=4)
+
+        def load_u(j):
+            nc.sync.dma_start(out=u_sb[j][:], in_=u_view[:, 2 * j : 2 * j + 2, :])
+
+        def zero_planes(r):
+            nc.vector.memset(h_planes[r][:].bitcast(I32), 0)
+            nc.vector.memset(w_planes[r][:].bitcast(I32), 0)
+
+        def load_scales(planes, src, r, q):
+            g0, g1 = RUNS[r]
+            nc.sync.dma_start(
+                out=planes[r][32 * q : 32 * q + 4, :, :].bitcast(I32),
+                in_=src[g0:g1, 4 * q : 4 * q + 4, :].rearrange("g r n -> r g n").bitcast(I32),
+            )
+
+        def load_run(r):
+            for q in range(4):
+                load_scales(h_planes, h_scales, r, q)
+            for q in range(4):
+                load_scales(w_planes, W_out_scales, r, q)
+
+        def load_codes(g):
+            nc.sync.dma_start(out=h_codes[g][:].bitcast(I32), in_=h_words[g].bitcast(I32))
+            for g0, g1 in W_LOADS:
+                if g0 == g:
+                    nc.sync.dma_start(
+                        out=w_codes[g][0][:].bitcast(I32),
+                        in_=W_out_words[g0:g1].rearrange("g p n -> p g n").bitcast(I32),
+                    )
+
+        nc.gpsimd.memset(zeros[:].bitcast(F32), 0.0)
+        make_identity(nc, ident[:])
+        nc.gpsimd.memset(ones[:], 1.0)
+        nc.gpsimd.memset(brow[:].bitcast(F32), 0.0)
+        zero_planes(0)
+        zero_planes(1)
+        nc.scalar.activation(out=junk[:], in_=zeros[:, 0:1], func=ACT.Gelu)
+
+        nc.sync.dma_start(
+            out=z_sb[:], in_=z.rearrange("b m p r -> (b m p) r").rearrange("(t p j) r -> p t (j r)", t=2, j=4)
+        )
+        load_u(0)
+        load_u(1)
+        for q in range(4):
+            load_scales(h_planes, h_scales, 0, q)
+        load_scales(w_planes, W_out_scales, 0, 0)
+        load_u(2)
+        load_u(3)
+        for q in range(1, 4):
+            load_scales(w_planes, W_out_scales, 0, q)
+        for g in range(RUNS[0][0], RUNS[0][1]):
+            load_codes(g)
+        nc.sync.dma_start(out=brow[0:1, :], in_=b.rearrange("b x y c -> (x y) (b c)"))
+        b_out_row = b_out.rearrange("(o c) -> o c", o=1)
+        nc.sync.dma_start(out=brow[1:2, 0:CH], in_=b_out_row)
+        nc.sync.dma_start(out=brow[1:2, CH : 2 * CH], in_=b_out_row)
+        load_run(1)
+        for g in range(RUNS[1][0], RUNS[1][1]):
+            load_codes(g)
+
+        warm_ps = bank(0, CH, F32, "warm_ps")
+        for k in range(WARM):
+            nc.tensor.matmul(out=warm_ps[:], lhsT=zeros[:, 0:P], rhs=zeros[:], start=True, stop=True)
+
+        for t in range(2):
+            zp = bank(1 + t, CH, BF16, "zT_ps%d" % t)
+            for j in range(4):
+                nc.tensor.matmul(
+                    out=zp[:, P * j : P * (j + 1)], lhsT=z_sb[:, t, P * j : P * (j + 1)], rhs=ident[:], start=True, stop=True
+                )
+            zT_half = zT[:, CH * t : CH * (t + 1)].rearrange("r (p j) -> r p j", j=4)
+            if t == 0:
+                nc.vector.tensor_copy(out=zT_half, in_=zp[:].rearrange("r (j p) -> r p j", j=4))
+            else:
+                nc.scalar.copy(out=zT_half, in_=zp[:].rearrange("r (j p) -> r p j", j=4))
+
+        uT = {}
+        lora = {}
+
+        def transpose_u(i, k):
+            up = bank(k, CH, BF16, "uT_ps%d" % i)
+            for e in range(4):
+                nc.tensor.matmul(
+                    out=up[:, P * e : P * (e + 1)],
+                    lhsT=u_sb[i // 2][:, i % 2, P * e : P * (e + 1)],
+                    rhs=ident[:],
+                    start=True,
+                    stop=True,
+                )
+            ut = keep.tile([P, CH], BF16, name="uT%d" % i)
+            if i % 2 == 0:
+                nc.vector.tensor_copy(out=ut[:], in_=up[:])
+            else:
+                nc.scalar.copy(out=ut[:], in_=up[:])
+            uT[i] = ut
+
+        def low_rank(i, k):
+            lp = bank(k, CH, F32, "lora_ps%d" % i)
+            nc.tensor.matmul(out=lp[:], lhsT=zT[:, P * i : P * (i + 1)], rhs=uT[i][:], start=True, stop=True)
+            lb = keep.tile([P, CH], F32, name="lora%d" % i)
+            if i % 2 == 1:
+                nc.scalar.activation(
+                    out=lb[:].rearrange("q (p e) -> q p e", e=4),
+                    in_=lp[:].rearrange("q (e p) -> q p e", e=4),
+                    func=ACT.Copy,
+                    scale=1.0 / RANK,
+                )
+            else:
+                nc.vector.tensor_scalar(
+                    out=lb[:].rearrange("q (p e) -> q p e", e=4),
+                    in0=lp[:].rearrange("q (e p) -> q p e", e=4),
+                    scalar1=1.0 / RANK,
+                    scalar2=None,
+                    op0=ALU.mult,
+                )
+            lora[i] = lb
+
+        for half in range(2):
+            for j in range(4):
+                transpose_u(4 * half + j, 3 + j)
+            for j in range(4):
+                low_rank(4 * half + j, (7 + j) % 8)
+
+        for r in range(2, len(RUNS)):
+            zero_planes(r)
+            load_run(r)
+            for g in range(RUNS[r][0], RUNS[r][1]):
+                load_codes(g)
+
+        def mx(acc, i, c0, c1, g):
+            r, k = run_of[g]
+            nc.tensor.matmul_mx(
+                out=acc[:],
+                lhsT=h_codes[g][:, 2 * P * i : 2 * P * (i + 1)].bitcast(FP4X4),
+                lhsT_scale=h_planes[r][:, k, P * i : P * (i + 1)],
+                rhs=w_codes[g][0][:, w_codes[g][1], 2 * c0 : 2 * c1].bitcast(FP4X4),
+                rhs_scale=w_planes[r][:, k, c0:c1],
+                start=(g == 0),
+                stop=(g == PASSES - 1),
+            )
+
+        out_rows = out.rearrange("b m p c -> (b m) p c")
+
+        def finish(acc, i, c0, c1, queue):
+            pre = work.tile([P, c1 - c0], F32, tag="pre", name="pre")
+            nc.vector.tensor_tensor(out=pre[:], in0=acc[:], in1=lora[i][:, c0:c1], op=ALU.add)
+            res = work.tile([P, c1 - c0], F32, tag="res", name="res")
+            nc.scalar.activation(out=res[:], in_=pre[:], func=ACT.Gelu)
+            queue.dma_start(out=out_rows[i][:, c0:c1], in_=res[:])
+
+        early = []
+        for i, k in enumerate((3, 4, 5, 6, 7, 0)):
+            a = bank(k, CH, F32, "acc%d" % i)
+            early.append((a, i, 0, CH))
+        for g in range(LATE - 1):
+            for grp in early:
+                mx(*grp, g)
+
+        for t in range(2):
+            bp = bank(1 + t, CH, F32, "bias_ps%d" % t)
+            nc.tensor.matmul(out=bp[:], lhsT=ones[:], rhs=brow[:, CH * t : CH * (t + 1)], start=True, stop=True)
+            if t == 0:
+                nc.vector.tensor_copy(out=bias_sb[:, t, :], in_=bp[:])
+            else:
+                nc.scalar.copy(out=bias_sb[:, t, :], in_=bp[:])
+        for i in range(TILES):
+            nc.vector.tensor_tensor(out=lora[i][:], in0=lora[i][:], in1=bias_sb[:, i // 4, :], op=ALU.add)
+
+        for grp in early:
+            mx(*grp, LATE - 1)
+        acc6 = bank(1, CH, F32, "acc6")
+        acc7a = bank(2, HALF, F32, "acc7a")
+        late = [(acc6, 6, 0, CH), (acc7a, 7, 0, HALF)]
+        for grp in late:
+            for g in range(LATE):
+                mx(*grp, g)
+
+        groups = early + late
+        for g in range(LATE, SWEEP):
+            for grp in groups:
+                mx(*grp, g)
+        for grp in groups:
+            for g in range(SWEEP, PASSES):
+                mx(*grp, g)
+            finish(*grp, nc.sync)
+        acc7b = bank(3, HALF, F32, "acc7b")
+        for g in range(PASSES):
+            mx(acc7b, 7, HALF, CH, g)
+        finish(acc7b, 7, HALF, CH, nc.scalar)

@@ -24,7 +24,6 @@ RUNS = ((0, 3), (3, 7), (7, 11), (11, 16))
 W_LOADS = ((0, 1), (1, 2), (2, 4), (4, 6), (6, 8), (8, 10), (10, 12), (12, 14), (14, 16))
 SWEEP = 13
 WARM = 3
-LATE = 3
 
 
 def tile_loratacmlp4_pb_kernel(tc, h_words, h_scales, z, u, b, W_out_words, W_out_scales, b_out, out):
@@ -39,9 +38,8 @@ def tile_loratacmlp4_pb_kernel(tc, h_words, h_scales, z, u, b, W_out_words, W_ou
             return psum.tile([P, width], dtype, tag="bank%d" % k, name=name)
 
         zeros = keep.tile([P, CH], BF16, name="zeros")
-        ones = keep.tile([P, P], BF16, name="ones")
         ident = keep.tile([P, P], BF16, name="ident")
-        brow = keep.tile([P, 2 * CH], BF16, name="brow")
+        bias_bc = keep.tile([P, 3, CH], BF16, name="bias_bc")
         junk = keep.tile([P, 1], F32, name="junk")
         z_sb = keep.tile([P, 2, CH], BF16, name="z_sb")
         zT = keep.tile([P, TILES * P], BF16, name="zT")
@@ -83,8 +81,8 @@ def tile_loratacmlp4_pb_kernel(tc, h_words, h_scales, z, u, b, W_out_words, W_ou
         def load_scales(planes, src, r, q):
             g0, g1 = RUNS[r]
             nc.sync.dma_start(
-                out=planes[r][32 * q : 32 * q + 4, :, :].bitcast(I32),
-                in_=src[g0:g1, 4 * q : 4 * q + 4, :].rearrange("g r n -> r g n").bitcast(I32),
+                out=planes[r][q : P : 32, :, :].bitcast(I32),
+                in_=src[g0:g1, q : 16 : 4, :].rearrange("g r n -> r g n").bitcast(I32),
             )
 
         def load_run(r):
@@ -104,8 +102,6 @@ def tile_loratacmlp4_pb_kernel(tc, h_words, h_scales, z, u, b, W_out_words, W_ou
 
         nc.gpsimd.memset(zeros[:].bitcast(F32), 0.0)
         make_identity(nc, ident[:])
-        nc.gpsimd.memset(ones[:], 1.0)
-        nc.gpsimd.memset(brow[:].bitcast(F32), 0.0)
         zero_planes(0)
         zero_planes(1)
         nc.scalar.activation(out=junk[:], in_=zeros[:, 0:1], func=ACT.Gelu)
@@ -124,10 +120,6 @@ def tile_loratacmlp4_pb_kernel(tc, h_words, h_scales, z, u, b, W_out_words, W_ou
             load_scales(w_planes, W_out_scales, 0, q)
         for g in range(RUNS[0][0], RUNS[0][1]):
             load_codes(g)
-        nc.sync.dma_start(out=brow[0:1, :], in_=b.rearrange("b x y c -> (x y) (b c)"))
-        b_out_row = b_out.rearrange("(o c) -> o c", o=1)
-        nc.sync.dma_start(out=brow[1:2, 0:CH], in_=b_out_row)
-        nc.sync.dma_start(out=brow[1:2, CH : 2 * CH], in_=b_out_row)
         load_run(1)
         for g in range(RUNS[1][0], RUNS[1][1]):
             load_codes(g)
@@ -197,9 +189,20 @@ def tile_loratacmlp4_pb_kernel(tc, h_words, h_scales, z, u, b, W_out_words, W_ou
 
         for r in range(2, len(RUNS)):
             zero_planes(r)
+        for r in range(2, len(RUNS)):
             load_run(r)
             for g in range(RUNS[r][0], RUNS[r][1]):
                 load_codes(g)
+            if r == 2:
+                nc.sync.dma_start(
+                    out=bias_bc[:, 0:2, :].rearrange("p t c -> p (t c)"),
+                    in_=b.rearrange("b x y c -> (b x y c)").partition_broadcast(P),
+                )
+                nc.sync.dma_start(out=bias_bc[:, 2, :], in_=b_out.partition_broadcast(P))
+        for t in range(2):
+            nc.vector.tensor_tensor(out=bias_sb[:, t, :], in0=bias_bc[:, t, :], in1=bias_bc[:, 2, :], op=ALU.add)
+        for i in range(TILES):
+            nc.vector.tensor_tensor(out=lora[i][:], in0=lora[i][:], in1=bias_sb[:, i // 4, :], op=ALU.add)
 
         def mx(acc, i, c0, c1, g):
             r, k = run_of[g]
@@ -222,35 +225,13 @@ def tile_loratacmlp4_pb_kernel(tc, h_words, h_scales, z, u, b, W_out_words, W_ou
             nc.scalar.activation(out=res[:], in_=pre[:], func=ACT.Gelu)
             queue.dma_start(out=out_rows[i][:, c0:c1], in_=res[:])
 
-        early = []
-        for i, k in enumerate((3, 4, 5, 6, 7, 0)):
+        groups = []
+        for i, k in enumerate((3, 4, 5, 6, 7, 0, 1)):
             a = bank(k, CH, F32, "acc%d" % i)
-            early.append((a, i, 0, CH))
-        for g in range(LATE - 1):
-            for grp in early:
-                mx(*grp, g)
-
-        for t in range(2):
-            bp = bank(1 + t, CH, F32, "bias_ps%d" % t)
-            nc.tensor.matmul(out=bp[:], lhsT=ones[:], rhs=brow[:, CH * t : CH * (t + 1)], start=True, stop=True)
-            if t == 0:
-                nc.vector.tensor_copy(out=bias_sb[:, t, :], in_=bp[:])
-            else:
-                nc.scalar.copy(out=bias_sb[:, t, :], in_=bp[:])
-        for i in range(TILES):
-            nc.vector.tensor_tensor(out=lora[i][:], in0=lora[i][:], in1=bias_sb[:, i // 4, :], op=ALU.add)
-
-        for grp in early:
-            mx(*grp, LATE - 1)
-        acc6 = bank(1, CH, F32, "acc6")
+            groups.append((a, i, 0, CH))
         acc7a = bank(2, HALF, F32, "acc7a")
-        late = [(acc6, 6, 0, CH), (acc7a, 7, 0, HALF)]
-        for grp in late:
-            for g in range(LATE):
-                mx(*grp, g)
-
-        groups = early + late
-        for g in range(LATE, SWEEP):
+        groups.append((acc7a, 7, 0, HALF))
+        for g in range(SWEEP):
             for grp in groups:
                 mx(*grp, g)
         for grp in groups:

@@ -30,7 +30,7 @@ def tile_loratacmlp4_pb_kernel(tc, h_words, h_scales, z, u, b, W_out_words, W_ou
     nc = tc.nc
     with ExitStack() as ctx:
         keep = ctx.enter_context(tc.tile_pool(name="keep", bufs=1))
-        work = ctx.enter_context(tc.tile_pool(name="work", bufs=3))
+        work = ctx.enter_context(tc.tile_pool(name="work", bufs=9))
         psum = ctx.enter_context(tc.psum_pool(name="psum", bufs=1))
         ctx.enter_context(tc.manual_schedule())
 

@@ -51,17 +51,17 @@ def tile_loratacmlp4_pb_kernel(tc, h_words, h_scales, z, u, b, W_out_words, W_ou
         h_planes = []
         w_planes = []
         for r, (g0, g1) in enumerate(RUNS):
-            hp = keep.tile([P, g1 - g0, ROWS], U8, name="h_planes%d" % r, align_bytes=64)
-            wp = keep.tile([P, g1 - g0, CH], U8, name="w_planes%d" % r, align_bytes=64)
+            hp = keep.tile([P, g1 - g0, ROWS], U8, name="h_planes%d" % r, align_bytes=256)
+            wp = keep.tile([P, g1 - g0, CH], U8, name="w_planes%d" % r, align_bytes=256)
             h_planes.append(hp)
             w_planes.append(wp)
         h_codes = []
         w_codes = []
         for g in range(PASSES):
-            hc = keep.tile([P, 2 * ROWS], U8, name="h_codes%d" % g, align_bytes=64)
+            hc = keep.tile([P, 2 * ROWS], U8, name="h_codes%d" % g, align_bytes=256)
             h_codes.append(hc)
         for g0, g1 in W_LOADS:
-            wc = keep.tile([P, g1 - g0, 2 * CH], U8, name="w_codes%d" % g0, align_bytes=64)
+            wc = keep.tile([P, g1 - g0, 2 * CH], U8, name="w_codes%d" % g0, align_bytes=256)
             for g in range(g0, g1):
                 w_codes.append((wc, g - g0))
         run_of = {}

@@ -45,9 +45,10 @@ def tile_loratacmlp4_pb_kernel(tc, h_words, h_scales, z, u, b, W_out_words, W_ou
         zT = keep.tile([P, TILES * P], BF16, name="zT")
         bias_sb = keep.tile([P, 2, CH], F32, name="bias_sb")
         u_sb = []
-        for j in range(TILES // 2):
+        for j in range(2):
             u_pair = keep.tile([P, 2, CH], BF16, name="u_sb%d" % j)
             u_sb.append(u_pair)
+        u_four = keep.tile([P, 4, CH], BF16, name="u_four")
         h_planes = []
         w_planes = []
         for r, (g0, g1) in enumerate(RUNS):
@@ -113,10 +114,8 @@ def tile_loratacmlp4_pb_kernel(tc, h_words, h_scales, z, u, b, W_out_words, W_ou
         load_u(1)
         for q in range(4):
             load_scales(h_planes, h_scales, 0, q)
-        load_scales(w_planes, W_out_scales, 0, 0)
-        load_u(2)
-        load_u(3)
-        for q in range(1, 4):
+        nc.sync.dma_start(out=u_four[:], in_=u_view[:, 4:8, :])
+        for q in range(4):
             load_scales(w_planes, W_out_scales, 0, q)
         for g in range(RUNS[0][0], RUNS[0][1]):
             load_codes(g)
@@ -148,7 +147,7 @@ def tile_loratacmlp4_pb_kernel(tc, h_words, h_scales, z, u, b, W_out_words, W_ou
             for e in range(4):
                 nc.tensor.matmul(
                     out=up[:, P * e : P * (e + 1)],
-                    lhsT=u_sb[i // 2][:, i % 2, P * e : P * (e + 1)],
+                    lhsT=(u_sb[i // 2][:, i % 2, P * e : P * (e + 1)] if i < 4 else u_four[:, i - 4, P * e : P * (e + 1)]),
                     rhs=ident[:],
                     start=True,
                     stop=True,

from contextlib import ExitStack

import concourse.mybir as mybir
from concourse.masks import make_identity

F32 = mybir.dt.float32
BF16 = mybir.dt.bfloat16
I32 = mybir.dt.int32
U8 = mybir.dt.uint8
FP4X4 = mybir.dt.float4_e2m1fn_x4
ACT = mybir.ActivationFunctionType
ALU = mybir.AluOpType

P = 128
TILES = 8
PASSES = 16
CH = 512
HALF = CH // 2
ROWS = 1024
RANK = 128
FLOPS = 2 * ROWS * 8192 * CH + 2 * ROWS * RANK * CH

RUNS = ((0, 3), (3, 7), (7, 11), (11, 16))
W_LOADS = ((0, 1), (1, 2), (2, 4), (4, 6), (6, 8), (8, 10), (10, 12), (12, 14), (14, 16))
SWEEP = 13
WARM = 3


def tile_loratacmlp4_pb_kernel(tc, h_words, h_scales, z, u, b, W_out_words, W_out_scales, b_out, out):
    nc = tc.nc
    with ExitStack() as ctx:
        keep = ctx.enter_context(tc.tile_pool(name="keep", bufs=1))
        work = ctx.enter_context(tc.tile_pool(name="work", bufs=9))
        psum = ctx.enter_context(tc.psum_pool(name="psum", bufs=1))
        ctx.enter_context(tc.manual_schedule())

        def bank(k, width, dtype, name):
            return psum.tile([P, width], dtype, tag="bank%d" % k, name=name)

        zeros = keep.tile([P, CH], BF16, name="zeros")
        ident = keep.tile([P, P], BF16, name="ident")
        bias_bc = keep.tile([P, 3, CH], BF16, name="bias_bc")
        junk = keep.tile([P, 1], F32, name="junk")
        z_sb = keep.tile([P, 2, CH], BF16, name="z_sb")
        zT = keep.tile([P, TILES * P], BF16, name="zT")
        bias_sb = keep.tile([P, 2, CH], F32, name="bias_sb")
        u_sb = []
        for j in range(2):
            u_pair = keep.tile([P, 2, CH], BF16, name="u_sb%d" % j)
            u_sb.append(u_pair)
        u_four = keep.tile([P, 4, CH], BF16, name="u_four")
        h_planes = []
        w_planes = []
        for r, (g0, g1) in enumerate(RUNS):
            hp = keep.tile([P, g1 - g0, ROWS], U8, name="h_planes%d" % r, align_bytes=256)
            wp = keep.tile([P, g1 - g0, CH], U8, name="w_planes%d" % r, align_bytes=256)
            h_planes.append(hp)
            w_planes.append(wp)
        h_codes = []
        w_codes = []
        for g in range(PASSES):
            hc = keep.tile([P, 2 * ROWS], U8, name="h_codes%d" % g, align_bytes=256)
            h_codes.append(hc)
        for g0, g1 in W_LOADS:
            wc = keep.tile([P, g1 - g0, 2 * CH], U8, name="w_codes%d" % g0, align_bytes=256)
            for g in range(g0, g1):
                w_codes.append((wc, g - g0))
        run_of = {}
        for r, (g0, g1) in enumerate(RUNS):
            for g in range(g0, g1):
                run_of[g] = (r, g - g0)

        u_view = u.rearrange("b m (p e) r -> p (b m) (e r)", e=4)

        def load_u(j):
            nc.sync.dma_start(out=u_sb[j][:], in_=u_view[:, 2 * j : 2 * j + 2, :])

        def zero_planes(r):
            nc.vector.memset(h_planes[r][:].bitcast(I32), 0)
            nc.vector.memset(w_planes[r][:].bitcast(I32), 0)

        def load_scales(planes, src, r, q):
            g0, g1 = RUNS[r]
            nc.sync.dma_start(
                out=planes[r][q : P : 32, :, :].bitcast(I32),
                in_=src[g0:g1, q : 16 : 4, :].rearrange("g r n -> r g n").bitcast(I32),
            )

        def load_run(r):
            for q in range(4):
                load_scales(h_planes, h_scales, r, q)
            for q in range(4):
                load_scales(w_planes, W_out_scales, r, q)

        def load_codes(g):
            nc.sync.dma_start(out=h_codes[g][:].bitcast(I32), in_=h_words[g].bitcast(I32))
            for g0, g1 in W_LOADS:
                if g0 == g:
                    nc.sync.dma_start(
                        out=w_codes[g][0][:].bitcast(I32),
                        in_=W_out_words[g0:g1].rearrange("g p n -> p g n").bitcast(I32),
                    )

        nc.gpsimd.memset(zeros[:].bitcast(F32), 0.0)
        make_identity(nc, ident[:])
        zero_planes(0)
        zero_planes(1)
        nc.scalar.activation(out=junk[:], in_=zeros[:, 0:1], func=ACT.Gelu)

        nc.sync.dma_start(
            out=z_sb[:], in_=z.rearrange("b m p r -> (b m p) r").rearrange("(t p j) r -> p t (j r)", t=2, j=4)
        )
        load_u(0)
        load_u(1)
        for q in range(4):
            load_scales(h_planes, h_scales, 0, q)
        nc.sync.dma_start(out=u_four[:], in_=u_view[:, 4:8, :])
        for q in range(4):
            load_scales(w_planes, W_out_scales, 0, q)
        for g in range(RUNS[0][0], RUNS[0][1]):
            load_codes(g)
        load_run(1)
        for g in range(RUNS[1][0], RUNS[1][1]):
            load_codes(g)

        warm_ps = bank(0, CH, F32, "warm_ps")
        for k in range(WARM):
            nc.tensor.matmul(out=warm_ps[:], lhsT=zeros[:, 0:P], rhs=zeros[:], start=True, stop=True)

        for t in range(2):
            zp = bank(1 + t, CH, BF16, "zT_ps%d" % t)
            for j in range(4):
                nc.tensor.matmul(
                    out=zp[:, P * j : P * (j + 1)], lhsT=z_sb[:, t, P * j : P * (j + 1)], rhs=ident[:], start=True, stop=True
                )
            zT_half = zT[:, CH * t : CH * (t + 1)].rearrange("r (p j) -> r p j", j=4)
            if t == 0:
                nc.vector.tensor_copy(out=zT_half, in_=zp[:].rearrange("r (j p) -> r p j", j=4))
            else:
                nc.scalar.copy(out=zT_half, in_=zp[:].rearrange("r (j p) -> r p j", j=4))

        uT = {}
        lora = {}

        def transpose_u(i, k):
            up = bank(k, CH, BF16, "uT_ps%d" % i)
            for e in range(4):
                nc.tensor.matmul(
                    out=up[:, P * e : P * (e + 1)],
                    lhsT=(u_sb[i // 2][:, i % 2, P * e : P * (e + 1)] if i < 4 else u_four[:, i - 4, P * e : P * (e + 1)]),
                    rhs=ident[:],
                    start=True,
                    stop=True,
                )
            ut = keep.tile([P, CH], BF16, name="uT%d" % i)
            if i % 2 == 0:
                nc.vector.tensor_copy(out=ut[:], in_=up[:])
            else:
                nc.scalar.copy(out=ut[:], in_=up[:])
            uT[i] = ut

        def low_rank(i, k):
            lp = bank(k, CH, F32, "lora_ps%d" % i)
            nc.tensor.matmul(out=lp[:], lhsT=zT[:, P * i : P * (i + 1)], rhs=uT[i][:], start=True, stop=True)
            lb = keep.tile([P, CH], F32, name="lora%d" % i)
            if i % 2 == 1:
                nc.scalar.activation(
                    out=lb[:].rearrange("q (p e) -> q p e", e=4),
                    in_=lp[:].rearrange("q (e p) -> q p e", e=4),
                    func=ACT.Copy,
                    scale=1.0 / RANK,
                )
            else:
                nc.vector.tensor_scalar(
                    out=lb[:].rearrange("q (p e) -> q p e", e=4),
                    in0=lp[:].rearrange("q (e p) -> q p e", e=4),
                    scalar1=1.0 / RANK,
                    scalar2=None,
                    op0=ALU.mult,
                )
            lora[i] = lb

        for half in range(2):
            for j in range(4):
                transpose_u(4 * half + j, 3 + j)
            for j in range(4):
                low_rank(4 * half + j, (7 + j) % 8)

        for r in range(2, len(RUNS)):
            zero_planes(r)
        for r in range(2, len(RUNS)):
            load_run(r)
            for g in range(RUNS[r][0], RUNS[r][1]):
                load_codes(g)
            if r == 2:
                nc.sync.dma_start(
                    out=bias_bc[:, 0:2, :].rearrange("p t c -> p (t c)"),
                    in_=b.rearrange("b x y c -> (b x y c)").partition_broadcast(P),
                )
                nc.sync.dma_start(out=bias_bc[:, 2, :], in_=b_out.partition_broadcast(P))
        for t in range(2):
            nc.vector.tensor_tensor(out=bias_sb[:, t, :], in0=bias_bc[:, t, :], in1=bias_bc[:, 2, :], op=ALU.add)
        for i in range(TILES):
            nc.vector.tensor_tensor(out=lora[i][:], in0=lora[i][:], in1=bias_sb[:, i // 4, :], op=ALU.add)

        def mx(acc, i, c0, c1, g):
            r, k = run_of[g]
            nc.tensor.matmul_mx(
                out=acc[:],
                lhsT=h_codes[g][:, 2 * P * i : 2 * P * (i + 1)].bitcast(FP4X4),
                lhsT_scale=h_planes[r][:, k, P * i : P * (i + 1)],
                rhs=w_codes[g][0][:, w_codes[g][1], 2 * c0 : 2 * c1].bitcast(FP4X4),
                rhs_scale=w_planes[r][:, k, c0:c1],
                start=(g == 0),
                stop=(g == PASSES - 1),
            )

        out_rows = out.rearrange("b m p c -> (b m) p c")

        def finish(acc, i, c0, c1, queue):
            pre = work.tile([P, c1 - c0], F32, tag="pre", name="pre")
            nc.vector.tensor_tensor(out=pre[:], in0=acc[:], in1=lora[i][:, c0:c1], op=ALU.add)
            res = work.tile([P, c1 - c0], F32, tag="res", name="res")
            nc.scalar.activation(out=res[:], in_=pre[:], func=ACT.Gelu)
            queue.dma_start(out=out_rows[i][:, c0:c1], in_=res[:])

        groups = []
        for i, k in enumerate((3, 4, 5, 6, 7, 0, 1)):
            a = bank(k, CH, F32, "acc%d" % i)
            groups.append((a, i, 0, CH))
        acc7a = bank(2, HALF, F32, "acc7a")
        groups.append((acc7a, 7, 0, HALF))
        for g in range(SWEEP):
            for grp in groups:
                mx(*grp, g)
        for grp in groups:
            for g in range(SWEEP, PASSES):
                mx(*grp, g)
            finish(*grp, nc.sync)
        acc7b = bank(3, HALF, F32, "acc7b")
        for g in range(PASSES):
            mx(acc7b, 7, HALF, CH, g)
        finish(acc7b, 7, HALF, CH, nc.scalar)
